import numpy as np
import ml_dtypes


def mxq(x, axis, fmt="e4m3"):
    dtype, down = {"e4m3": (ml_dtypes.float8_e4m3fn, 7), "e5m2": (ml_dtypes.float8_e5m2, 14)}[fmt]
    v = np.moveaxis(np.asarray(x, np.float32).astype(ml_dtypes.bfloat16).astype(np.float64), axis, -1)
    blocks = v.reshape(v.shape[:-1] + (-1, 32))
    amax = np.abs(blocks).max(-1, keepdims=True)
    byte = np.maximum(np.where(amax > 0, np.frexp(amax)[1] - 1 + 127, 0) - down, 1)
    scale = np.exp2(byte - 127.0)
    codes = (blocks / scale).astype(np.float32).astype(dtype).astype(np.float64)
    return np.moveaxis((codes * scale).reshape(v.shape), -1, axis)


WIDE = False


def mx_kscale(k):
    if not WIDE:
        return np.ones(k)
    levels = np.array([10, -10, 5, -5, 0])
    a = np.random.permutation(np.resize(levels, k // 512 * 4)).reshape(k // 512, 4)
    idx = np.arange(k)
    return np.exp2(a[idx // 512, idx % 128 // 32])


BF16 = ml_dtypes.bfloat16


def bf(x):
    return np.asarray(x, np.float32).astype(BF16)


def f64(x):
    return np.asarray(x).astype(np.float64)


B, C, N, T, Q = 1, 128, 1024, 8, 4


def setup_inputs():
    s = mx_kscale(N)
    a = 2.0 / np.sqrt(N)
    return {"x": bf(np.random.standard_normal((B, C, N, T)) * s[:, None]),
            "Ar": bf(np.random.uniform(0.0, 1.0, (N, N)) * a / s),
            "Ai": bf(np.random.uniform(0.0, 1.0, (N, N)) * a / s),
            "Aj": bf(np.random.uniform(0.0, 1.0, (N, N)) * a / s),
            "Ak": bf(np.random.uniform(0.0, 1.0, (N, N)) * a / s)}


def reference(x, Ar, Ai, Aj, Ak):
    xq = mxq(f64(x), 2, "e4m3")
    Yr = mxq(f64(Ar), 1, "e4m3") @ xq
    Yi = mxq(f64(Ai), 1, "e4m3") @ xq
    Yj = mxq(f64(Aj), 1, "e4m3") @ xq
    Yk = mxq(f64(Ak), 1, "e4m3") @ xq
    Yr_r, Yr_i, Yr_j, Yr_k = np.split(Yr, Q, axis=1)
    Yi_r, Yi_i, Yi_j, Yi_k = np.split(Yi, Q, axis=1)
    Yj_r, Yj_i, Yj_j, Yj_k = np.split(Yj, Q, axis=1)
    Yk_r, Yk_i, Yk_j, Yk_k = np.split(Yk, Q, axis=1)
    out_r = Yr_r - Yi_i - Yj_j - Yk_k
    out_i = Yr_i + Yi_r + Yj_k - Yk_j
    out_j = Yr_j - Yi_k + Yj_r + Yk_i
    out_k = Yr_k + Yi_j - Yj_i + Yk_r
    return np.concatenate([out_r, out_i, out_j, out_k], axis=1)

@@ -1,0 +1,157 @@
+from contextlib import ExitStack
+
+import concourse.mybir as mybir
+from concourse.masks import make_identity
+
+F32 = mybir.dt.float32
+BF16 = mybir.dt.bfloat16
+U32 = mybir.dt.uint32
+U8 = mybir.dt.uint8
+FP8X4 = mybir.dt.float8_e4m3fn_x4
+
+P = 128
+PACK = 4
+K_PASS = P * PACK
+CHANNELS = 128
+GROUP = 32
+NODES = 1024
+STEPS = 8
+PASSES = NODES // K_PASS
+ADJ = 4
+BLOCK = 256
+BLOCKS = NODES // BLOCK
+SUB = BLOCK // P
+PAIRS = STEPS // 2
+BANK = 512
+
+FLOPS = 2 * ADJ * NODES * NODES * CHANNELS * STEPS
+
+HAMILTON = (
+    ((0, 1.0), (1, -1.0), (2, -1.0), (3, -1.0)),
+    ((1, 1.0), (0, 1.0), (3, 1.0), (2, -1.0)),
+    ((2, 1.0), (3, -1.0), (0, 1.0), (1, 1.0)),
+    ((3, 1.0), (2, 1.0), (1, -1.0), (0, 1.0)),
+)
+
+
+def tile_nconv_pa_kernel(tc, x, Ar, Ai, Aj, Ak, out):
+    nc = tc.nc
+    adjacency = (Ar, Ai, Aj, Ak)
+    x_rows = x.rearrange("b c m t -> (b c) (m t)")
+    out_rows = out.rearrange("b c n t -> (b c) (n t)")
+
+    with ExitStack() as pools:
+        keep = pools.enter_context(tc.tile_pool(name="keep", bufs=1))
+        x_stage = pools.enter_context(tc.tile_pool(name="x_stage", bufs=2))
+        a_load = pools.enter_context(tc.tile_pool(name="a_load", bufs=8))
+        a_stage = pools.enter_context(tc.tile_pool(name="a_stage", bufs=4))
+        flipped = pools.enter_context(tc.psum_pool(name="flipped", bufs=4))
+        sums = pools.enter_context(tc.psum_pool(name="sums", bufs=4))
+
+        identity = keep.tile([P, P], F32, name="identity")
+        make_identity(nc, identity[:])
+
+        x_sb = keep.tile([P, NODES * STEPS], BF16, name="x_sb")
+        half = NODES * STEPS // PASSES
+        for g in range(PASSES):
+            nc.sync.dma_start(out=x_sb[:, g * half : (g + 1) * half], in_=x_rows[:, g * half : (g + 1) * half])
+        x_words = x_sb[:].bitcast(F32).rearrange(
+            "c (g h q e w) -> c g h q e w", g=PASSES, h=2, q=P, e=2, w=PAIRS
+        )
+
+        x_codes = [keep.tile([P, ADJ * PASSES * 2 * CHANNELS], U32, name="x_codes%d" % w, align_bytes=64) for w in range(PAIRS)]
+        x_scales = [keep.tile([P, ADJ * PASSES * 2 * CHANNELS], U8, name="x_scales%d" % w, align_bytes=64) for w in range(PAIRS)]
+        a_codes = [[keep.tile([P, PASSES * BLOCK], U32, name="a_codes%d_%d" % (b, a), align_bytes=64) for a in range(ADJ)] for b in range(BLOCKS)]
+        a_scales = [[keep.tile([P, PASSES * BLOCK], U8, name="a_scales%d_%d" % (b, a), align_bytes=64) for a in range(ADJ)] for b in range(BLOCKS)]
+        result = [keep.tile([P, BLOCK * STEPS], F32, name="result%d" % b) for b in range(BLOCKS)]
+
+        def prepare_x(w):
+            grouped = x_stage.tile([P, ADJ * PASSES * 2 * CHANNELS * PACK], BF16, tag="x_grouped", align_bytes=64)
+            by_adj = grouped[:].rearrange("p (a s k) -> p a s k", a=ADJ, s=PASSES * 2, k=CHANNELS * PACK)
+            for g in range(PASSES):
+                bank = flipped.tile([P, BANK], F32, tag="bank")
+                for h in range(2):
+                    for e in range(2):
+                        j = 2 * h + e
+                        nc.tensor.transpose(bank[:, j * P : (j + 1) * P], x_words[:, g, h, :, e, w], identity[:])
+                nc.scalar.copy(
+                    out=by_adj[:, 0, 2 * g : 2 * g + 2, :].rearrange("p o (c j) -> p o c j", j=PACK),
+                    in_=bank[:].bitcast(BF16).rearrange("p (j c o) -> p o c j", j=PACK, c=CHANNELS, o=2),
+                )
+            width = GROUP * PACK
+            for a in range(1, ADJ):
+                for group in range(4):
+                    source, sign = HAMILTON[group][a]
+                    nc.vector.tensor_scalar_mul(
+                        out=by_adj[:, a, :, group * width : (group + 1) * width],
+                        in0=by_adj[:, 0, :, source * width : (source + 1) * width],
+                        scalar1=sign,
+                    )
+            words = ADJ * PASSES * 2 * CHANNELS // 2
+            for piece in range(2):
+                nc.vector.quantize_mx(
+                    out=x_codes[w][:, piece * words : (piece + 1) * words].bitcast(FP8X4),
+                    scales=x_scales[w][:, piece * words : (piece + 1) * words],
+                    in_=grouped[:, piece * words * PACK : (piece + 1) * words * PACK],
+                )
+
+        def prepare_a(b, a):
+            rows = a_load.tile([P, SUB * NODES], BF16, tag="a_rows")
+            nc.sync.dma_start(
+                out=rows[:].rearrange("p (s m) -> p s m", s=SUB),
+                in_=adjacency[a][b * BLOCK : (b + 1) * BLOCK, :].rearrange("(s p) m -> p s m", p=P),
+            )
+            row_words = rows[:].bitcast(F32)
+            grouped = a_stage.tile([P, PASSES * BLOCK * PACK], BF16, tag="a_grouped", align_bytes=64)
+            grouped_words = grouped[:].bitcast(F32).rearrange("p (g s r h) -> p g s r h", g=PASSES, s=SUB, r=P, h=2)
+            for g in range(PASSES):
+                bank = flipped.tile([P, BANK], F32, tag="bank")
+                for s in range(SUB):
+                    for h in range(2):
+                        first = s * (NODES // 2) + (2 * g + h) * P
+                        nc.tensor.transpose(
+                            bank[:, (2 * s + h) * P : (2 * s + h + 1) * P], row_words[:, first : first + P], identity[:]
+                        )
+                nc.scalar.copy(
+                    out=grouped_words[:, g, :, :, :],
+                    in_=bank[:].rearrange("p (s h r) -> p s r h", s=SUB, h=2, r=P),
+                )
+            nc.vector.quantize_mx(out=a_codes[b][a][:].bitcast(FP8X4), scales=a_scales[b][a][:], in_=grouped[:])
+
+        def multiply(w, b):
+            acc = sums.tile([P, BANK], F32, tag="acc")
+            for o in range(2):
+                for a in range(ADJ):
+                    for g in range(PASSES):
+                        first = ((a * PASSES + g) * 2 + o) * CHANNELS
+                        nc.tensor.matmul_mx(
+                            out=acc[:, o * BLOCK : (o + 1) * BLOCK],
+                            lhsT=x_codes[w][:, first : first + CHANNELS].bitcast(FP8X4),
+                            lhsT_scale=x_scales[w][:, first : first + CHANNELS],
+                            rhs=a_codes[b][a][:, g * BLOCK : (g + 1) * BLOCK].bitcast(FP8X4),
+                            rhs_scale=a_scales[b][a][:, g * BLOCK : (g + 1) * BLOCK],
+                            start=(a == 0 and g == 0),
+                            stop=(a == ADJ - 1 and g == PASSES - 1),
+                        )
+            target = result[b][:].rearrange("c (n t) -> c n t", t=STEPS)[:, :, 2 * w : 2 * w + 2]
+            source = acc[:].rearrange("c (o n) -> c n o", o=2)
+            if b % 2 == 0:
+                nc.vector.tensor_copy(out=target, in_=source)
+            else:
+                nc.scalar.copy(out=target, in_=source)
+
+        prepare_x(0)
+        for a in range(ADJ):
+            prepare_a(0, a)
+        for w in range(PAIRS):
+            for b in range(BLOCKS):
+                if w == 0 and b + 1 < BLOCKS:
+                    for a in range(ADJ):
+                        prepare_a(b + 1, a)
+                if b == 0 and w + 1 < PAIRS:
+                    prepare_x(w + 1)
+                multiply(w, b)
+                if w == PAIRS - 1:
+                    nc.sync.dma_start(
+                        out=out_rows[:, b * BLOCK * STEPS : (b + 1) * BLOCK * STEPS], in_=result[b][:]
+                    )

@@ -13,7 +13,8 @@ P = 128
 PACK = 4
 K_PASS = P * PACK
 CHANNELS = 128
-GROUP = 32
+GROUPS = 4
+GROUP = CHANNELS // GROUPS
 NODES = 1024
 STEPS = 8
 PASSES = NODES // K_PASS
@@ -23,6 +24,9 @@ BLOCKS = NODES // BLOCK
 SUB = BLOCK // P
 PAIRS = STEPS // 2
 BANK = 512
+HALVES = 2
+
+X_COLS = ADJ * PASSES * 2 * CHANNELS
 
 FLOPS = 2 * ADJ * NODES * NODES * CHANNELS * STEPS
 
@@ -40,59 +44,78 @@ def tile_nconv_pa_kernel(tc, x, Ar, Ai, Aj, Ak, out):
     x_rows = x.rearrange("b c m t -> (b c) (m t)")
     out_rows = out.rearrange("b c n t -> (b c) (n t)")
 
-    with ExitStack() as pools:
-        keep = pools.enter_context(tc.tile_pool(name="keep", bufs=1))
-        x_stage = pools.enter_context(tc.tile_pool(name="x_stage", bufs=2))
-        a_load = pools.enter_context(tc.tile_pool(name="a_load", bufs=8))
-        a_stage = pools.enter_context(tc.tile_pool(name="a_stage", bufs=4))
-        flipped = pools.enter_context(tc.psum_pool(name="flipped", bufs=4))
-        sums = pools.enter_context(tc.psum_pool(name="sums", bufs=4))
+    with ExitStack() as stack:
+        keep = stack.enter_context(tc.tile_pool(name="keep", bufs=1))
+        x_stage = stack.enter_context(tc.tile_pool(name="x_stage", bufs=2))
+        a_load = stack.enter_context(tc.tile_pool(name="a_load", bufs=8))
+        a_stage = stack.enter_context(tc.tile_pool(name="a_stage", bufs=6))
+        flipped = stack.enter_context(tc.psum_pool(name="flipped", bufs=4))
+        sums = stack.enter_context(tc.psum_pool(name="sums", bufs=4))
+        stack.enter_context(tc.manual_schedule())
 
         identity = keep.tile([P, P], F32, name="identity")
         make_identity(nc, identity[:])
 
         x_sb = keep.tile([P, NODES * STEPS], BF16, name="x_sb")
-        half = NODES * STEPS // PASSES
+        x_half = NODES * STEPS // PASSES
         for g in range(PASSES):
-            nc.sync.dma_start(out=x_sb[:, g * half : (g + 1) * half], in_=x_rows[:, g * half : (g + 1) * half])
-        x_words = x_sb[:].bitcast(F32).rearrange(
-            "c (g h q e w) -> c g h q e w", g=PASSES, h=2, q=P, e=2, w=PAIRS
-        )
+            nc.sync.dma_start(out=x_sb[:, g * x_half : (g + 1) * x_half], in_=x_rows[:, g * x_half : (g + 1) * x_half])
+        x_words = x_sb[:].bitcast(F32).rearrange("c (g h q e w) -> c g h q e w", g=PASSES, h=2, q=P, e=2, w=PAIRS)
 
-        x_codes = [keep.tile([P, ADJ * PASSES * 2 * CHANNELS], U32, name="x_codes%d" % w, align_bytes=64) for w in range(PAIRS)]
-        x_scales = [keep.tile([P, ADJ * PASSES * 2 * CHANNELS], U8, name="x_scales%d" % w, align_bytes=64) for w in range(PAIRS)]
-        a_codes = [[keep.tile([P, PASSES * BLOCK], U32, name="a_codes%d_%d" % (b, a), align_bytes=64) for a in range(ADJ)] for b in range(BLOCKS)]
-        a_scales = [[keep.tile([P, PASSES * BLOCK], U8, name="a_scales%d_%d" % (b, a), align_bytes=64) for a in range(ADJ)] for b in range(BLOCKS)]
+        x_codes = [keep.tile([P, X_COLS], U32, name="x_codes%d" % w, align_bytes=64) for w in range(PAIRS)]
+        x_scales = [keep.tile([P, X_COLS], U8, name="x_scales%d" % w, align_bytes=64) for w in range(PAIRS)]
+        a_codes = [
+            [keep.tile([P, PASSES * BLOCK], U32, name="a_codes%d_%d" % (b, a), align_bytes=64) for a in range(ADJ)]
+            for b in range(BLOCKS)
+        ]
+        a_scales = [
+            [keep.tile([P, PASSES * BLOCK], U8, name="a_scales%d_%d" % (b, a), align_bytes=64) for a in range(ADJ)]
+            for b in range(BLOCKS)
+        ]
         result = [keep.tile([P, BLOCK * STEPS], F32, name="result%d" % b) for b in range(BLOCKS)]
+        x_banks = {}
+        x_grouped = {}
+        sum_banks = {}
 
-        def prepare_x(w):
-            grouped = x_stage.tile([P, ADJ * PASSES * 2 * CHANNELS * PACK], BF16, tag="x_grouped", align_bytes=64)
-            by_adj = grouped[:].rearrange("p (a s k) -> p a s k", a=ADJ, s=PASSES * 2, k=CHANNELS * PACK)
+        def by_component(w):
+            return x_grouped[w][:].rearrange("p (a s k) -> p a s k", a=ADJ, s=PASSES * 2, k=CHANNELS * PACK)
+
+        def flip_x(w):
             for g in range(PASSES):
                 bank = flipped.tile([P, BANK], F32, tag="bank")
+                x_banks[(w, g)] = bank
                 for h in range(2):
                     for e in range(2):
                         j = 2 * h + e
                         nc.tensor.transpose(bank[:, j * P : (j + 1) * P], x_words[:, g, h, :, e, w], identity[:])
+
+        def sort_x(w):
+            grouped = x_stage.tile([P, X_COLS * PACK], BF16, tag="x_grouped", align_bytes=64)
+            x_grouped[w] = grouped
+            for g in range(PASSES):
                 nc.scalar.copy(
-                    out=by_adj[:, 0, 2 * g : 2 * g + 2, :].rearrange("p o (c j) -> p o c j", j=PACK),
-                    in_=bank[:].bitcast(BF16).rearrange("p (j c o) -> p o c j", j=PACK, c=CHANNELS, o=2),
+                    out=by_component(w)[:, 0, 2 * g : 2 * g + 2, :].rearrange("p o (c j) -> p o c j", j=PACK),
+                    in_=x_banks[(w, g)][:].bitcast(BF16).rearrange("p (j c o) -> p o c j", j=PACK, c=CHANNELS, o=2),
                 )
+
+        def sign_x(w):
             width = GROUP * PACK
             for a in range(1, ADJ):
-                for group in range(4):
+                for group in range(GROUPS):
                     source, sign = HAMILTON[group][a]
                     nc.vector.tensor_scalar_mul(
-                        out=by_adj[:, a, :, group * width : (group + 1) * width],
-                        in0=by_adj[:, 0, :, source * width : (source + 1) * width],
+                        out=by_component(w)[:, a, :, group * width : (group + 1) * width],
+                        in0=by_component(w)[:, 0, :, source * width : (source + 1) * width],
                         scalar1=sign,
                     )
-            words = ADJ * PASSES * 2 * CHANNELS // 2
+
+        def quantise_x(w):
+            words = X_COLS // 2
             for piece in range(2):
                 nc.vector.quantize_mx(
                     out=x_codes[w][:, piece * words : (piece + 1) * words].bitcast(FP8X4),
                     scales=x_scales[w][:, piece * words : (piece + 1) * words],
-                    in_=grouped[:, piece * words * PACK : (piece + 1) * words * PACK],
+                    in_=x_grouped[w][:, piece * words * PACK : (piece + 1) * words * PACK],
                 )
 
         def prepare_a(b, a):
@@ -119,13 +142,14 @@ def tile_nconv_pa_kernel(tc, x, Ar, Ai, Aj, Ak, out):
             nc.vector.quantize_mx(out=a_codes[b][a][:].bitcast(FP8X4), scales=a_scales[b][a][:], in_=grouped[:])
 
         def multiply(w, b):
-            acc = sums.tile([P, BANK], F32, tag="acc")
+            bank = sums.tile([P, BANK], F32, tag="sum_bank")
+            sum_banks[(w, b)] = bank
             for o in range(2):
                 for a in range(ADJ):
                     for g in range(PASSES):
                         first = ((a * PASSES + g) * 2 + o) * CHANNELS
                         nc.tensor.matmul_mx(
-                            out=acc[:, o * BLOCK : (o + 1) * BLOCK],
+                            out=bank[:, o * BLOCK : (o + 1) * BLOCK],
                             lhsT=x_codes[w][:, first : first + CHANNELS].bitcast(FP8X4),
                             lhsT_scale=x_scales[w][:, first : first + CHANNELS],
                             rhs=a_codes[b][a][:, g * BLOCK : (g + 1) * BLOCK].bitcast(FP8X4),
@@ -133,25 +157,44 @@ def tile_nconv_pa_kernel(tc, x, Ar, Ai, Aj, Ak, out):
                             start=(a == 0 and g == 0),
                             stop=(a == ADJ - 1 and g == PASSES - 1),
                         )
-            target = result[b][:].rearrange("c (n t) -> c n t", t=STEPS)[:, :, 2 * w : 2 * w + 2]
-            source = acc[:].rearrange("c (o n) -> c n o", o=2)
-            if b % 2 == 0:
-                nc.vector.tensor_copy(out=target, in_=source)
-            else:
-                nc.scalar.copy(out=target, in_=source)
 
-        prepare_x(0)
+        def empty(w, b):
+            nodes = BLOCK // HALVES
+            for half in range(HALVES):
+                target = result[b][:].rearrange("c (n t) -> c n t", t=STEPS)
+                source = sum_banks[(w, b)][:].rearrange("c (o n) -> c n o", o=2)
+                copy = nc.vector.tensor_copy if b % 2 == 0 else nc.scalar.copy
+                copy(
+                    out=target[:, half * nodes : (half + 1) * nodes, 2 * w : 2 * w + 2],
+                    in_=source[:, half * nodes : (half + 1) * nodes, :],
+                )
+                if w == PAIRS - 1:
+                    first = (b * BLOCK + half * nodes) * STEPS
+                    nc.sync.dma_start(
+                        out=out_rows[:, first : first + nodes * STEPS],
+                        in_=result[b][:, half * nodes * STEPS : (half + 1) * nodes * STEPS],
+                    )
+
+        flip_x(0)
+        sort_x(0)
+        sign_x(0)
+        quantise_x(0)
         for a in range(ADJ):
             prepare_a(0, a)
-        for w in range(PAIRS):
-            for b in range(BLOCKS):
-                if w == 0 and b + 1 < BLOCKS:
-                    for a in range(ADJ):
-                        prepare_a(b + 1, a)
-                if b == 0 and w + 1 < PAIRS:
-                    prepare_x(w + 1)
-                multiply(w, b)
-                if w == PAIRS - 1:
-                    nc.sync.dma_start(
-                        out=out_rows[:, b * BLOCK * STEPS : (b + 1) * BLOCK * STEPS], in_=result[b][:]
-                    )
+        steps = [(w, b) for w in range(PAIRS) for b in range(BLOCKS)]
+        for i, (w, b) in enumerate(steps):
+            if w == 0 and b + 1 < BLOCKS:
+                for a in range(ADJ):
+                    prepare_a(b + 1, a)
+            if w + 1 < PAIRS:
+                if b == 0:
+                    flip_x(w + 1)
+                    sort_x(w + 1)
+                if b == 1:
+                    sign_x(w + 1)
+                if b == 2:
+                    quantise_x(w + 1)
+            multiply(w, b)
+            if i > 0:
+                empty(*steps[i - 1])
+        empty(*steps[-1])

@@ -5,9 +5,11 @@ from concourse.masks import make_identity
 
 F32 = mybir.dt.float32
 BF16 = mybir.dt.bfloat16
+I32 = mybir.dt.int32
 U32 = mybir.dt.uint32
 U8 = mybir.dt.uint8
 FP8X4 = mybir.dt.float8_e4m3fn_x4
+COPY = mybir.ActivationFunctionType.Copy
 
 P = 128
 PACK = 4
@@ -24,9 +26,13 @@ BLOCKS = NODES // BLOCK
 SUB = BLOCK // P
 PAIRS = STEPS // 2
 BANK = 512
-HALVES = 2
 
-X_COLS = ADJ * PASSES * 2 * CHANNELS
+SLOTS = PASSES * 2
+SRC_COLS = SLOTS * 2 * CHANNELS
+CHAIN = 6
+WIN_COLS = SLOTS * CHAIN * GROUP
+
+RUN = 2
 
 FLOPS = 2 * ADJ * NODES * NODES * CHANNELS * STEPS
 
@@ -38,11 +44,22 @@ HAMILTON = (
 )
 
 
+ROW_SIGN = (1.0, 1.0, 1.0, -1.0)
+
+
+def slot_of(group, a):
+    source, sign = HAMILTON[group][a]
+    return source + (GROUPS if sign * ROW_SIGN[group] == ROW_SIGN[source] else 0)
+
+
 def tile_nconv_pa_kernel(tc, x, Ar, Ai, Aj, Ak, out):
     nc = tc.nc
     adjacency = (Ar, Ai, Aj, Ak)
     x_rows = x.rearrange("b c m t -> (b c) (m t)")
     out_rows = out.rearrange("b c n t -> (b c) (n t)")
+    windows = [[slot_of(group, a) for group in range(GROUPS)] for a in range(ADJ)]
+    assert windows[0] == [4, 5, 6, 7] and windows[2] == [2, 3, 4, 5] and windows[1][2:] == windows[3][:2]
+    chain_slots = windows[1] + windows[3][2:]
 
     with ExitStack() as stack:
         keep = stack.enter_context(tc.tile_pool(name="keep", bufs=1))
@@ -62,8 +79,15 @@ def tile_nconv_pa_kernel(tc, x, Ar, Ai, Aj, Ak, out):
             nc.sync.dma_start(out=x_sb[:, g * x_half : (g + 1) * x_half], in_=x_rows[:, g * x_half : (g + 1) * x_half])
         x_words = x_sb[:].bitcast(F32).rearrange("c (g h q e w) -> c g h q e w", g=PASSES, h=2, q=P, e=2, w=PAIRS)
 
-        x_codes = [keep.tile([P, X_COLS], U32, name="x_codes%d" % w, align_bytes=64) for w in range(PAIRS)]
-        x_scales = [keep.tile([P, X_COLS], U8, name="x_scales%d" % w, align_bytes=64) for w in range(PAIRS)]
+        src_codes = [keep.tile([P, SRC_COLS], I32, name="src_codes%d" % w, align_bytes=64) for w in range(PAIRS)]
+        src_scales = [keep.tile([P, SRC_COLS], U8, name="src_scales%d" % w, align_bytes=64) for w in range(PAIRS)]
+        win_codes = [keep.tile([P, WIN_COLS], I32, name="win_codes%d" % w, align_bytes=64) for w in range(PAIRS)]
+        win_scales = [keep.tile([P, WIN_COLS], U8, name="win_scales%d" % w, align_bytes=64) for w in range(PAIRS)]
+        row_sign = keep.tile([P, 1], F32, name="row_sign")
+        for group in range(GROUPS):
+            nc.vector.memset(row_sign[group * GROUP : (group + 1) * GROUP, :], ROW_SIGN[group])
+        for w in range(PAIRS):
+            nc.vector.memset(src_scales[w][:].bitcast(I32), 0)
         a_codes = [
             [keep.tile([P, PASSES * BLOCK], U32, name="a_codes%d_%d" % (b, a), align_bytes=64) for a in range(ADJ)]
             for b in range(BLOCKS)
@@ -73,128 +97,217 @@ def tile_nconv_pa_kernel(tc, x, Ar, Ai, Aj, Ak, out):
             for b in range(BLOCKS)
         ]
         result = [keep.tile([P, BLOCK * STEPS], F32, name="result%d" % b) for b in range(BLOCKS)]
+        a_rows = {}
+        a_banks = {}
+        a_grouped = {}
         x_banks = {}
         x_grouped = {}
         sum_banks = {}
 
-        def by_component(w):
-            return x_grouped[w][:].rearrange("p (a s k) -> p a s k", a=ADJ, s=PASSES * 2, k=CHANNELS * PACK)
+        def by_sign(w):
+            return x_grouped[w][:].rearrange("p (s v k) -> p s v k", s=SLOTS, v=2, k=CHANNELS * PACK)
 
-        def flip_x(w):
-            for g in range(PASSES):
-                bank = flipped.tile([P, BANK], F32, tag="bank")
-                x_banks[(w, g)] = bank
-                for h in range(2):
-                    for e in range(2):
-                        j = 2 * h + e
-                        nc.tensor.transpose(bank[:, j * P : (j + 1) * P], x_words[:, g, h, :, e, w], identity[:])
-
-        def sort_x(w):
-            grouped = x_stage.tile([P, X_COLS * PACK], BF16, tag="x_grouped", align_bytes=64)
-            x_grouped[w] = grouped
-            for g in range(PASSES):
-                nc.scalar.copy(
-                    out=by_component(w)[:, 0, 2 * g : 2 * g + 2, :].rearrange("p o (c j) -> p o c j", j=PACK),
-                    in_=x_banks[(w, g)][:].bitcast(BF16).rearrange("p (j c o) -> p o c j", j=PACK, c=CHANNELS, o=2),
-                )
-
-        def sign_x(w):
-            width = GROUP * PACK
-            for a in range(1, ADJ):
-                for group in range(GROUPS):
-                    source, sign = HAMILTON[group][a]
-                    nc.vector.tensor_scalar_mul(
-                        out=by_component(w)[:, a, :, group * width : (group + 1) * width],
-                        in0=by_component(w)[:, 0, :, source * width : (source + 1) * width],
-                        scalar1=sign,
-                    )
-
-        def quantise_x(w):
-            words = X_COLS // 2
-            for piece in range(2):
-                nc.vector.quantize_mx(
-                    out=x_codes[w][:, piece * words : (piece + 1) * words].bitcast(FP8X4),
-                    scales=x_scales[w][:, piece * words : (piece + 1) * words],
-                    in_=x_grouped[w][:, piece * words * PACK : (piece + 1) * words * PACK],
-                )
-
-        def prepare_a(b, a):
+        def load_a(b, a):
             rows = a_load.tile([P, SUB * NODES], BF16, tag="a_rows")
+            a_rows[(b, a)] = rows
             nc.sync.dma_start(
                 out=rows[:].rearrange("p (s m) -> p s m", s=SUB),
                 in_=adjacency[a][b * BLOCK : (b + 1) * BLOCK, :].rearrange("(s p) m -> p s m", p=P),
             )
-            row_words = rows[:].bitcast(F32)
-            grouped = a_stage.tile([P, PASSES * BLOCK * PACK], BF16, tag="a_grouped", align_bytes=64)
-            grouped_words = grouped[:].bitcast(F32).rearrange("p (g s r h) -> p g s r h", g=PASSES, s=SUB, r=P, h=2)
+
+        def flip_x(w, g):
+            bank = flipped.tile([P, BANK], F32, tag="bank")
+            x_banks[(w, g)] = bank
+            for h in range(2):
+                for e in range(2):
+                    j = 2 * h + e
+                    nc.tensor.transpose(bank[:, j * P : (j + 1) * P], x_words[:, g, h, :, e, w], identity[:])
+
+        def sort_x(w, g, on_vector):
+            if g == 0:
+                x_grouped[w] = x_stage.tile([P, SRC_COLS * PACK], BF16, tag="x_grouped", name="x_grouped", align_bytes=64)
+            target = by_sign(w)[:, 2 * g : 2 * g + 2, 1, :].rearrange("p o (c j) -> p o c j", j=PACK)
+            source = x_banks[(w, g)][:].bitcast(BF16).rearrange("p (j c o) -> p o c j", j=PACK, c=CHANNELS, o=2)
+            plus = GROUP * 3
+            if on_vector:
+                nc.vector.tensor_copy(out=target[:, :, :plus, :], in_=source[:, :, :plus, :])
+                nc.vector.tensor_scalar_mul(out=target[:, :, plus:, :], in0=source[:, :, plus:, :], scalar1=-1.0)
+            else:
+                nc.scalar.copy(out=target[:, :, :plus, :], in_=source[:, :, :plus, :])
+                nc.scalar.activation(out=target[:, :, plus:, :], in_=source[:, :, plus:, :], func=COPY, scale=-1.0)
+
+        def negate_x(w):
+            nc.vector.tensor_scalar_mul(out=by_sign(w)[:, :, 0, :], in0=by_sign(w)[:, :, 1, :], scalar1=-1.0)
+
+        def quantise_x(w):
+            nc.vector.quantize_mx(out=src_codes[w][:].bitcast(FP8X4), scales=src_scales[w][:], in_=x_grouped[w][:])
+
+        runs = []
+        for slot in chain_slots:
+            if runs and (slot > runs[-1][-1] if len(runs[-1]) == 1 else slot - runs[-1][-1] == runs[-1][1] - runs[-1][0]):
+                runs[-1].append(slot)
+            else:
+                runs.append([slot])
+
+        def permute_x(w):
+            for bytes_of_column, source_tile, window_tile in ((4, src_codes[w], win_codes[w]), (1, src_scales[w], win_scales[w])):
+                words = GROUP * bytes_of_column // 4
+                source_view = source_tile[:].bitcast(I32).rearrange("p (s q i) -> p s q i", s=SLOTS, q=2 * GROUPS, i=words)
+                window_view = window_tile[:].bitcast(I32).rearrange("p (s q i) -> p s q i", s=SLOTS, q=CHAIN, i=words)
+                position = 0
+                for run in runs:
+                    step = run[1] - run[0] if len(run) > 1 else 1
+                    nc.vector.tensor_copy(
+                        out=window_view[:, :, position : position + len(run), :],
+                        in_=source_view[:, :, run[0] : run[-1] + 1 : step, :],
+                    )
+                    position += len(run)
+
+        def flip_a(b, a):
+            row_words = a_rows[(b, a)][:].bitcast(F32)
             for g in range(PASSES):
                 bank = flipped.tile([P, BANK], F32, tag="bank")
+                a_banks[(b, a, g)] = bank
                 for s in range(SUB):
                     for h in range(2):
                         first = s * (NODES // 2) + (2 * g + h) * P
                         nc.tensor.transpose(
                             bank[:, (2 * s + h) * P : (2 * s + h + 1) * P], row_words[:, first : first + P], identity[:]
                         )
+
+        def sort_a(b, a):
+            grouped = a_stage.tile([P, PASSES * BLOCK * PACK], BF16, tag="a_grouped", align_bytes=64)
+            a_grouped[(b, a)] = grouped
+            grouped_words = grouped[:].bitcast(F32).rearrange("p (g s r h) -> p g s r h", g=PASSES, s=SUB, r=P, h=2)
+            for g in range(PASSES):
                 nc.scalar.copy(
                     out=grouped_words[:, g, :, :, :],
-                    in_=bank[:].rearrange("p (s h r) -> p s r h", s=SUB, h=2, r=P),
+                    in_=a_banks[(b, a, g)][:].rearrange("p (s h r) -> p s r h", s=SUB, h=2, r=P),
                 )
-            nc.vector.quantize_mx(out=a_codes[b][a][:].bitcast(FP8X4), scales=a_scales[b][a][:], in_=grouped[:])
 
-        def multiply(w, b):
+        def quantise_a(b, a):
+            nc.vector.quantize_mx(out=a_codes[b][a][:].bitcast(FP8X4), scales=a_scales[b][a][:], in_=a_grouped[(b, a)][:])
+
+        def multiply(w, b, first_node=0, nodes=BLOCK):
             bank = sums.tile([P, BANK], F32, tag="sum_bank")
-            sum_banks[(w, b)] = bank
+            sum_banks[(w, b, first_node)] = bank
             for o in range(2):
                 for a in range(ADJ):
                     for g in range(PASSES):
-                        first = ((a * PASSES + g) * 2 + o) * CHANNELS
+                        s = 2 * g + o
+                        if a % 2 == 0:
+                            codes, scales, first = src_codes[w], src_scales[w], (2 * GROUPS * s + windows[a][0]) * GROUP
+                        else:
+                            codes, scales, first = win_codes[w], win_scales[w], (CHAIN * s + a - 1) * GROUP
+                        moving = g * BLOCK + first_node
                         nc.tensor.matmul_mx(
-                            out=bank[:, o * BLOCK : (o + 1) * BLOCK],
-                            lhsT=x_codes[w][:, first : first + CHANNELS].bitcast(FP8X4),
-                            lhsT_scale=x_scales[w][:, first : first + CHANNELS],
-                            rhs=a_codes[b][a][:, g * BLOCK : (g + 1) * BLOCK].bitcast(FP8X4),
-                            rhs_scale=a_scales[b][a][:, g * BLOCK : (g + 1) * BLOCK],
+                            out=bank[:, o * nodes : (o + 1) * nodes],
+                            lhsT=codes[:, first : first + CHANNELS].bitcast(FP8X4),
+                            lhsT_scale=scales[:, first : first + CHANNELS],
+                            rhs=a_codes[b][a][:, moving : moving + nodes].bitcast(FP8X4),
+                            rhs_scale=a_scales[b][a][:, moving : moving + nodes],
                             start=(a == 0 and g == 0),
                             stop=(a == ADJ - 1 and g == PASSES - 1),
                         )
 
-        def empty(w, b):
-            nodes = BLOCK // HALVES
-            for half in range(HALVES):
-                target = result[b][:].rearrange("c (n t) -> c n t", t=STEPS)
-                source = sum_banks[(w, b)][:].rearrange("c (o n) -> c n o", o=2)
-                copy = nc.vector.tensor_copy if b % 2 == 0 else nc.scalar.copy
-                copy(
-                    out=target[:, half * nodes : (half + 1) * nodes, 2 * w : 2 * w + 2],
-                    in_=source[:, half * nodes : (half + 1) * nodes, :],
-                )
+        def empty(w, b, on_vector, first_node=0, nodes=BLOCK, pieces=1):
+            target = result[b][:].rearrange("c (n t) -> c n t", t=STEPS)
+            source = sum_banks[(w, b, first_node)][:, : 2 * nodes].rearrange("c (o n) -> c n o", o=2)
+            piece = nodes // pieces
+            for i in range(pieces):
+                to = target[:, first_node + i * piece : first_node + (i + 1) * piece, 2 * w : 2 * w + 2]
+                if on_vector:
+                    nc.vector.tensor_scalar_mul(out=to, in0=source[:, i * piece : (i + 1) * piece, :], scalar1=row_sign[:, 0:1])
+                else:
+                    nc.scalar.activation(out=to, in_=source[:, i * piece : (i + 1) * piece, :], func=COPY, scale=row_sign[:, 0:1])
                 if w == PAIRS - 1:
-                    first = (b * BLOCK + half * nodes) * STEPS
-                    nc.sync.dma_start(
-                        out=out_rows[:, first : first + nodes * STEPS],
-                        in_=result[b][:, half * nodes * STEPS : (half + 1) * nodes * STEPS],
-                    )
+                    store(b, first_node + i * piece, piece)
 
-        flip_x(0)
-        sort_x(0)
-        sign_x(0)
+        def store(b, first_node, nodes):
+            first = (b * BLOCK + first_node) * STEPS
+            nc.sync.dma_start(
+                out=out_rows[:, first : first + nodes * STEPS],
+                in_=result[b][:, first_node * STEPS : (first_node + nodes) * STEPS],
+            )
+
+        for b in range(BLOCKS):
+            for a in range(ADJ):
+                load_a(b, a)
+
+        for g in range(PASSES):
+            flip_x(0, g)
+            flip_x(1, g)
+            sort_x(0, g, False)
+            sort_x(1, g, True)
+        flip_a(0, 0)
+        sort_a(0, 0)
+        negate_x(0)
+        flip_a(0, 1)
+        sort_a(0, 1)
         quantise_x(0)
-        for a in range(ADJ):
-            prepare_a(0, a)
-        steps = [(w, b) for w in range(PAIRS) for b in range(BLOCKS)]
-        for i, (w, b) in enumerate(steps):
-            if w == 0 and b + 1 < BLOCKS:
-                for a in range(ADJ):
-                    prepare_a(b + 1, a)
-            if w + 1 < PAIRS:
-                if b == 0:
-                    flip_x(w + 1)
-                    sort_x(w + 1)
-                if b == 1:
-                    sign_x(w + 1)
-                if b == 2:
-                    quantise_x(w + 1)
-            multiply(w, b)
+        quantise_a(0, 0)
+        flip_a(0, 2)
+        sort_a(0, 2)
+        permute_x(0)
+        quantise_a(0, 1)
+        flip_a(0, 3)
+        sort_a(0, 3)
+        quantise_a(0, 2)
+        quantise_a(0, 3)
+        negate_x(1)
+
+        units = [("a", 1, a) for a in range(ADJ)]
+        for i in range(2, PAIRS):
+            units.append(("x", i, 0))
+            units.extend(("a", i, a) for a in range(ADJ))
+        steps = []
+        for i in range(PAIRS):
+            steps.extend((i, b) for b in range(i))
+            steps.extend((w, i) for w in range(i + 1))
+
+        def flip(unit):
+            kind, i, a = unit
+            if kind == "x":
+                for g in range(PASSES):
+                    flip_x(i, g)
+            else:
+                flip_a(i, a)
+
+        def sort(unit):
+            kind, i, a = unit
+            if kind == "x":
+                for g in range(PASSES):
+                    sort_x(i, g, False)
+            else:
+                sort_a(i, a)
+
+        def finish(unit):
+            kind, i, a = unit
+            if kind == "x":
+                negate_x(i)
+                quantise_x(i)
+                permute_x(i)
+            else:
+                quantise_a(i, a)
+
+        last = len(steps) - 1
+        for i, step in enumerate(steps):
+            run = units[RUN * i : RUN * (i + 1)]
+            for unit in run:
+                flip(unit)
+            for unit in run:
+                sort(unit)
+            if i == 0:
+                quantise_x(1)
+                permute_x(1)
+            if i < last:
+                multiply(*step)
+            else:
+                multiply(*step, first_node=0, nodes=BLOCK // 2)
             if i > 0:
-                empty(*steps[i - 1])
-        empty(*steps[-1])
+                empty(*steps[i - 1], on_vector=(i % 2 == 0 or RUN * i < len(units)))
+            for unit in run:
+                finish(unit)
+        multiply(*steps[last], first_node=BLOCK // 2, nodes=BLOCK // 2)
+        empty(*steps[last], on_vector=True, first_node=0, nodes=BLOCK // 2)
+        empty(*steps[last], on_vector=False, first_node=BLOCK // 2, nodes=BLOCK // 2, pieces=2)

@@ -115,8 +115,11 @@ def tile_nconv_pa_kernel(tc, x, Ar, Ai, Aj, Ak, out):
                 in_=adjacency[a][b * BLOCK : (b + 1) * BLOCK, :].rearrange("(s p) m -> p s m", p=P),
             )
 
-        def flip_x(w, g):
-            bank = flipped.tile([P, BANK], F32, tag="bank")
+        def flip_x(w, g, parked=False):
+            if parked:
+                bank = sums.tile([P, BANK], F32, tag="sum_bank")
+            else:
+                bank = flipped.tile([P, BANK], F32, tag="bank")
             x_banks[(w, g)] = bank
             for h in range(2):
                 for e in range(2):
@@ -242,10 +245,12 @@ def tile_nconv_pa_kernel(tc, x, Ar, Ai, Aj, Ak, out):
         flip_a(0, 0)
         sort_a(0, 0)
         negate_x(0)
+        flip_x(2, 0, parked=True)
         flip_a(0, 1)
         sort_a(0, 1)
         quantise_x(0)
         quantise_a(0, 0)
+        flip_x(2, 1, parked=True)
         flip_a(0, 2)
         sort_a(0, 2)
         permute_x(0)
@@ -256,10 +261,9 @@ def tile_nconv_pa_kernel(tc, x, Ar, Ai, Aj, Ak, out):
         quantise_a(0, 3)
         negate_x(1)
 
-        units = [("a", 1, a) for a in range(ADJ)]
-        for i in range(2, PAIRS):
-            units.append(("x", i, 0))
-            units.extend(("a", i, a) for a in range(ADJ))
+        units = [("a", 1, a) for a in range(ADJ)] + [("a", 2, a) for a in range(ADJ)]
+        units.append(("x", 3, 0))
+        units.extend(("a", 3, a) for a in range(ADJ))
         steps = []
         for i in range(PAIRS):
             steps.extend((i, b) for b in range(i))
@@ -300,6 +304,7 @@ def tile_nconv_pa_kernel(tc, x, Ar, Ai, Aj, Ak, out):
             if i == 0:
                 quantise_x(1)
                 permute_x(1)
+                sort(("x", 2, 0))
             if i < last:
                 multiply(*step)
             else:
@@ -308,6 +313,8 @@ def tile_nconv_pa_kernel(tc, x, Ar, Ai, Aj, Ak, out):
                 empty(*steps[i - 1], on_vector=(i % 2 == 0 or RUN * i < len(units)))
             for unit in run:
                 finish(unit)
+            if i == 1:
+                finish(("x", 2, 0))
         multiply(*steps[last], first_node=BLOCK // 2, nodes=BLOCK // 2)
         empty(*steps[last], on_vector=True, first_node=0, nodes=BLOCK // 2)
         empty(*steps[last], on_vector=False, first_node=BLOCK // 2, nodes=BLOCK // 2, pieces=2)

@@ -26,6 +26,7 @@ BLOCKS = NODES // BLOCK
 SUB = BLOCK // P
 PAIRS = STEPS // 2
 BANK = 512
+BANKS = 8
 
 SLOTS = PASSES * 2
 SRC_COLS = SLOTS * 2 * CHANNELS
@@ -63,12 +64,23 @@ def tile_nconv_pa_kernel(tc, x, Ar, Ai, Aj, Ak, out):
 
     with ExitStack() as stack:
         keep = stack.enter_context(tc.tile_pool(name="keep", bufs=1))
-        x_stage = stack.enter_context(tc.tile_pool(name="x_stage", bufs=2))
+        x_stage = stack.enter_context(tc.tile_pool(name="x_stage", bufs=3))
         a_load = stack.enter_context(tc.tile_pool(name="a_load", bufs=8))
         a_stage = stack.enter_context(tc.tile_pool(name="a_stage", bufs=6))
-        flipped = stack.enter_context(tc.psum_pool(name="flipped", bufs=4))
-        sums = stack.enter_context(tc.psum_pool(name="sums", bufs=4))
+        psum = stack.enter_context(tc.psum_pool(name="psum", bufs=1))
         stack.enter_context(tc.manual_schedule())
+
+        free_banks = list(range(BANKS))
+        bank_of = {}
+
+        def take_bank(key):
+            assert free_banks, "more than eight tiles alive in PSUM"
+            bank_of[key] = free_banks[0]
+            free_banks.remove(free_banks[0])
+            return psum.tile([P, BANK], F32, tag="bank%d" % bank_of[key], name="bank%d" % bank_of[key])
+
+        def give_back(key):
+            free_banks.append(bank_of[key])
 
         identity = keep.tile([P, P], F32, name="identity")
         make_identity(nc, identity[:])
@@ -115,11 +127,8 @@ def tile_nconv_pa_kernel(tc, x, Ar, Ai, Aj, Ak, out):
                 in_=adjacency[a][b * BLOCK : (b + 1) * BLOCK, :].rearrange("(s p) m -> p s m", p=P),
             )
 
-        def flip_x(w, g, parked=False):
-            if parked:
-                bank = sums.tile([P, BANK], F32, tag="sum_bank")
-            else:
-                bank = flipped.tile([P, BANK], F32, tag="bank")
+        def flip_x(w, g):
+            bank = take_bank(("x", w, g))
             x_banks[(w, g)] = bank
             for h in range(2):
                 for e in range(2):
@@ -138,6 +147,7 @@ def tile_nconv_pa_kernel(tc, x, Ar, Ai, Aj, Ak, out):
             else:
                 nc.scalar.copy(out=target[:, :, :plus, :], in_=source[:, :, :plus, :])
                 nc.scalar.activation(out=target[:, :, plus:, :], in_=source[:, :, plus:, :], func=COPY, scale=-1.0)
+            give_back(("x", w, g))
 
         def negate_x(w):
             nc.vector.tensor_scalar_mul(out=by_sign(w)[:, :, 0, :], in0=by_sign(w)[:, :, 1, :], scalar1=-1.0)
@@ -169,7 +179,7 @@ def tile_nconv_pa_kernel(tc, x, Ar, Ai, Aj, Ak, out):
         def flip_a(b, a):
             row_words = a_rows[(b, a)][:].bitcast(F32)
             for g in range(PASSES):
-                bank = flipped.tile([P, BANK], F32, tag="bank")
+                bank = take_bank(("a", b, a, g))
                 a_banks[(b, a, g)] = bank
                 for s in range(SUB):
                     for h in range(2):
@@ -187,12 +197,13 @@ def tile_nconv_pa_kernel(tc, x, Ar, Ai, Aj, Ak, out):
                     out=grouped_words[:, g, :, :, :],
                     in_=a_banks[(b, a, g)][:].rearrange("p (s h r) -> p s r h", s=SUB, h=2, r=P),
                 )
+                give_back(("a", b, a, g))
 
         def quantise_a(b, a):
             nc.vector.quantize_mx(out=a_codes[b][a][:].bitcast(FP8X4), scales=a_scales[b][a][:], in_=a_grouped[(b, a)][:])
 
         def multiply(w, b, first_node=0, nodes=BLOCK):
-            bank = sums.tile([P, BANK], F32, tag="sum_bank")
+            bank = take_bank(("sum", w, b, first_node))
             sum_banks[(w, b, first_node)] = bank
             for o in range(2):
                 for a in range(ADJ):
@@ -225,6 +236,7 @@ def tile_nconv_pa_kernel(tc, x, Ar, Ai, Aj, Ak, out):
                     nc.scalar.activation(out=to, in_=source[:, i * piece : (i + 1) * piece, :], func=COPY, scale=row_sign[:, 0:1])
                 if w == PAIRS - 1:
                     store(b, first_node + i * piece, piece)
+            give_back(("sum", w, b, first_node))
 
         def store(b, first_node, nodes):
             first = (b * BLOCK + first_node) * STEPS
@@ -245,24 +257,25 @@ def tile_nconv_pa_kernel(tc, x, Ar, Ai, Aj, Ak, out):
         flip_a(0, 0)
         sort_a(0, 0)
         negate_x(0)
-        flip_x(2, 0, parked=True)
+        flip_x(2, 0)
         flip_a(0, 1)
         sort_a(0, 1)
         quantise_x(0)
         quantise_a(0, 0)
-        flip_x(2, 1, parked=True)
+        flip_x(2, 1)
         flip_a(0, 2)
         sort_a(0, 2)
         permute_x(0)
         quantise_a(0, 1)
+        flip_x(3, 0)
         flip_a(0, 3)
         sort_a(0, 3)
+        flip_x(3, 1)
         quantise_a(0, 2)
         quantise_a(0, 3)
         negate_x(1)
 
         units = [("a", 1, a) for a in range(ADJ)] + [("a", 2, a) for a in range(ADJ)]
-        units.append(("x", 3, 0))
         units.extend(("a", 3, a) for a in range(ADJ))
         steps = []
         for i in range(PAIRS):
@@ -315,6 +328,9 @@ def tile_nconv_pa_kernel(tc, x, Ar, Ai, Aj, Ak, out):
                 finish(unit)
             if i == 1:
                 finish(("x", 2, 0))
+                sort(("x", 3, 0))
+            if i == 3:
+                finish(("x", 3, 0))
         multiply(*steps[last], first_node=BLOCK // 2, nodes=BLOCK // 2)
         empty(*steps[last], on_vector=True, first_node=0, nodes=BLOCK // 2)
         empty(*steps[last], on_vector=False, first_node=BLOCK // 2, nodes=BLOCK // 2, pieces=2)

from contextlib import ExitStack

import concourse.mybir as mybir
from concourse.masks import make_identity

F32 = mybir.dt.float32
BF16 = mybir.dt.bfloat16
I32 = mybir.dt.int32
U32 = mybir.dt.uint32
U8 = mybir.dt.uint8
FP8X4 = mybir.dt.float8_e4m3fn_x4
COPY = mybir.ActivationFunctionType.Copy

P = 128
PACK = 4
K_PASS = P * PACK
CHANNELS = 128
GROUPS = 4
GROUP = CHANNELS // GROUPS
NODES = 1024
STEPS = 8
PASSES = NODES // K_PASS
ADJ = 4
BLOCK = 256
BLOCKS = NODES // BLOCK
SUB = BLOCK // P
PAIRS = STEPS // 2
BANK = 512
BANKS = 8

SLOTS = PASSES * 2
SRC_COLS = SLOTS * 2 * CHANNELS
CHAIN = 6
WIN_COLS = SLOTS * CHAIN * GROUP

RUN = 2

FLOPS = 2 * ADJ * NODES * NODES * CHANNELS * STEPS

HAMILTON = (
    ((0, 1.0), (1, -1.0), (2, -1.0), (3, -1.0)),
    ((1, 1.0), (0, 1.0), (3, 1.0), (2, -1.0)),
    ((2, 1.0), (3, -1.0), (0, 1.0), (1, 1.0)),
    ((3, 1.0), (2, 1.0), (1, -1.0), (0, 1.0)),
)


ROW_SIGN = (1.0, 1.0, 1.0, -1.0)


def slot_of(group, a):
    source, sign = HAMILTON[group][a]
    return source + (GROUPS if sign * ROW_SIGN[group] == ROW_SIGN[source] else 0)


def tile_nconv_pa_kernel(tc, x, Ar, Ai, Aj, Ak, out):
    nc = tc.nc
    adjacency = (Ar, Ai, Aj, Ak)
    x_rows = x.rearrange("b c m t -> (b c) (m t)")
    out_rows = out.rearrange("b c n t -> (b c) (n t)")
    windows = [[slot_of(group, a) for group in range(GROUPS)] for a in range(ADJ)]
    assert windows[0] == [4, 5, 6, 7] and windows[2] == [2, 3, 4, 5] and windows[1][2:] == windows[3][:2]
    chain_slots = windows[1] + windows[3][2:]

    with ExitStack() as stack:
        keep = stack.enter_context(tc.tile_pool(name="keep", bufs=1))
        x_stage = stack.enter_context(tc.tile_pool(name="x_stage", bufs=3))
        a_load = stack.enter_context(tc.tile_pool(name="a_load", bufs=8))
        a_stage = stack.enter_context(tc.tile_pool(name="a_stage", bufs=6))
        psum = stack.enter_context(tc.psum_pool(name="psum", bufs=1))
        stack.enter_context(tc.manual_schedule())

        free_banks = list(range(BANKS))
        bank_of = {}

        def take_bank(key):
            assert free_banks, "more than eight tiles alive in PSUM"
            bank_of[key] = free_banks[0]
            free_banks.remove(free_banks[0])
            return psum.tile([P, BANK], F32, tag="bank%d" % bank_of[key], name="bank%d" % bank_of[key])

        def give_back(key):
            free_banks.append(bank_of[key])

        identity = keep.tile([P, P], F32, name="identity")
        make_identity(nc, identity[:])

        x_sb = keep.tile([P, NODES * STEPS], BF16, name="x_sb")
        x_half = NODES * STEPS // PASSES
        for g in range(PASSES):
            nc.sync.dma_start(out=x_sb[:, g * x_half : (g + 1) * x_half], in_=x_rows[:, g * x_half : (g + 1) * x_half])
        x_words = x_sb[:].bitcast(F32).rearrange("c (g h q e w) -> c g h q e w", g=PASSES, h=2, q=P, e=2, w=PAIRS)

        src_codes = [keep.tile([P, SRC_COLS], I32, name="src_codes%d" % w, align_bytes=64) for w in range(PAIRS)]
        src_scales = [keep.tile([P, SRC_COLS], U8, name="src_scales%d" % w, align_bytes=64) for w in range(PAIRS)]
        win_codes = [keep.tile([P, WIN_COLS], I32, name="win_codes%d" % w, align_bytes=64) for w in range(PAIRS)]
        win_scales = [keep.tile([P, WIN_COLS], U8, name="win_scales%d" % w, align_bytes=64) for w in range(PAIRS)]
        row_sign = keep.tile([P, 1], F32, name="row_sign")
        for group in range(GROUPS):
            nc.vector.memset(row_sign[group * GROUP : (group + 1) * GROUP, :], ROW_SIGN[group])
        for w in range(PAIRS):
            nc.vector.memset(src_scales[w][:].bitcast(I32), 0)
        a_codes = [
            [keep.tile([P, PASSES * BLOCK], U32, name="a_codes%d_%d" % (b, a), align_bytes=64) for a in range(ADJ)]
            for b in range(BLOCKS)
        ]
        a_scales = [
            [keep.tile([P, PASSES * BLOCK], U8, name="a_scales%d_%d" % (b, a), align_bytes=64) for a in range(ADJ)]
            for b in range(BLOCKS)
        ]
        result = [keep.tile([P, BLOCK * STEPS], F32, name="result%d" % b) for b in range(BLOCKS)]
        a_rows = {}
        a_banks = {}
        a_grouped = {}
        x_banks = {}
        x_grouped = {}
        sum_banks = {}

        def by_sign(w):
            return x_grouped[w][:].rearrange("p (s v k) -> p s v k", s=SLOTS, v=2, k=CHANNELS * PACK)

        def load_a(b, a):
            rows = a_load.tile([P, SUB * NODES], BF16, tag="a_rows")
            a_rows[(b, a)] = rows
            nc.sync.dma_start(
                out=rows[:].rearrange("p (s m) -> p s m", s=SUB),
                in_=adjacency[a][b * BLOCK : (b + 1) * BLOCK, :].rearrange("(s p) m -> p s m", p=P),
            )

        def flip_x(w, g):
            bank = take_bank(("x", w, g))
            x_banks[(w, g)] = bank
            for h in range(2):
                for e in range(2):
                    j = 2 * h + e
                    nc.tensor.transpose(bank[:, j * P : (j + 1) * P], x_words[:, g, h, :, e, w], identity[:])

        def sort_x(w, g, on_vector):
            if g == 0:
                x_grouped[w] = x_stage.tile([P, SRC_COLS * PACK], BF16, tag="x_grouped", name="x_grouped", align_bytes=64)
            target = by_sign(w)[:, 2 * g : 2 * g + 2, 1, :].rearrange("p o (c j) -> p o c j", j=PACK)
            source = x_banks[(w, g)][:].bitcast(BF16).rearrange("p (j c o) -> p o c j", j=PACK, c=CHANNELS, o=2)
            plus = GROUP * 3
            if on_vector:
                nc.vector.tensor_copy(out=target[:, :, :plus, :], in_=source[:, :, :plus, :])
                nc.vector.tensor_scalar_mul(out=target[:, :, plus:, :], in0=source[:, :, plus:, :], scalar1=-1.0)
            else:
                nc.scalar.copy(out=target[:, :, :plus, :], in_=source[:, :, :plus, :])
                nc.scalar.activation(out=target[:, :, plus:, :], in_=source[:, :, plus:, :], func=COPY, scale=-1.0)
            give_back(("x", w, g))

        def negate_x(w):
            nc.vector.tensor_scalar_mul(out=by_sign(w)[:, :, 0, :], in0=by_sign(w)[:, :, 1, :], scalar1=-1.0)

        def quantise_x(w):
            nc.vector.quantize_mx(out=src_codes[w][:].bitcast(FP8X4), scales=src_scales[w][:], in_=x_grouped[w][:])

        runs = []
        for slot in chain_slots:
            if runs and (slot > runs[-1][-1] if len(runs[-1]) == 1 else slot - runs[-1][-1] == runs[-1][1] - runs[-1][0]):
                runs[-1].append(slot)
            else:
                runs.append([slot])

        def permute_x(w):
            for bytes_of_column, source_tile, window_tile in ((4, src_codes[w], win_codes[w]), (1, src_scales[w], win_scales[w])):
                words = GROUP * bytes_of_column // 4
                source_view = source_tile[:].bitcast(I32).rearrange("p (s q i) -> p s q i", s=SLOTS, q=2 * GROUPS, i=words)
                window_view = window_tile[:].bitcast(I32).rearrange("p (s q i) -> p s q i", s=SLOTS, q=CHAIN, i=words)
                position = 0
                for run in runs:
                    step = run[1] - run[0] if len(run) > 1 else 1
                    nc.vector.tensor_copy(
                        out=window_view[:, :, position : position + len(run), :],
                        in_=source_view[:, :, run[0] : run[-1] + 1 : step, :],
                    )
                    position += len(run)

        def flip_a(b, a):
            row_words = a_rows[(b, a)][:].bitcast(F32)
            for g in range(PASSES):
                bank = take_bank(("a", b, a, g))
                a_banks[(b, a, g)] = bank
                for s in range(SUB):
                    for h in range(2):
                        first = s * (NODES // 2) + (2 * g + h) * P
                        nc.tensor.transpose(
                            bank[:, (2 * s + h) * P : (2 * s + h + 1) * P], row_words[:, first : first + P], identity[:]
                        )

        def sort_a(b, a):
            grouped = a_stage.tile([P, PASSES * BLOCK * PACK], BF16, tag="a_grouped", align_bytes=64)
            a_grouped[(b, a)] = grouped
            grouped_words = grouped[:].bitcast(F32).rearrange("p (g s r h) -> p g s r h", g=PASSES, s=SUB, r=P, h=2)
            for g in range(PASSES):
                nc.scalar.copy(
                    out=grouped_words[:, g, :, :, :],
                    in_=a_banks[(b, a, g)][:].rearrange("p (s h r) -> p s r h", s=SUB, h=2, r=P),
                )
                give_back(("a", b, a, g))

        def quantise_a(b, a):
            nc.vector.quantize_mx(out=a_codes[b][a][:].bitcast(FP8X4), scales=a_scales[b][a][:], in_=a_grouped[(b, a)][:])

        def multiply(w, b, first_node=0, nodes=BLOCK):
            bank = take_bank(("sum", w, b, first_node))
            sum_banks[(w, b, first_node)] = bank
            for o in range(2):
                for a in range(ADJ):
                    for g in range(PASSES):
                        s = 2 * g + o
                        if a % 2 == 0:
                            codes, scales, first = src_codes[w], src_scales[w], (2 * GROUPS * s + windows[a][0]) * GROUP
                        else:
                            codes, scales, first = win_codes[w], win_scales[w], (CHAIN * s + a - 1) * GROUP
                        moving = g * BLOCK + first_node
                        nc.tensor.matmul_mx(
                            out=bank[:, o * nodes : (o + 1) * nodes],
                            lhsT=codes[:, first : first + CHANNELS].bitcast(FP8X4),
                            lhsT_scale=scales[:, first : first + CHANNELS],
                            rhs=a_codes[b][a][:, moving : moving + nodes].bitcast(FP8X4),
                            rhs_scale=a_scales[b][a][:, moving : moving + nodes],
                            start=(a == 0 and g == 0),
                            stop=(a == ADJ - 1 and g == PASSES - 1),
                        )

        def empty(w, b, on_vector, first_node=0, nodes=BLOCK, pieces=1):
            target = result[b][:].rearrange("c (n t) -> c n t", t=STEPS)
            source = sum_banks[(w, b, first_node)][:, : 2 * nodes].rearrange("c (o n) -> c n o", o=2)
            piece = nodes // pieces
            for i in range(pieces):
                to = target[:, first_node + i * piece : first_node + (i + 1) * piece, 2 * w : 2 * w + 2]
                if on_vector:
                    nc.vector.tensor_scalar_mul(out=to, in0=source[:, i * piece : (i + 1) * piece, :], scalar1=row_sign[:, 0:1])
                else:
                    nc.scalar.activation(out=to, in_=source[:, i * piece : (i + 1) * piece, :], func=COPY, scale=row_sign[:, 0:1])
                if w == PAIRS - 1:
                    store(b, first_node + i * piece, piece)
            give_back(("sum", w, b, first_node))

        def store(b, first_node, nodes):
            first = (b * BLOCK + first_node) * STEPS
            nc.sync.dma_start(
                out=out_rows[:, first : first + nodes * STEPS],
                in_=result[b][:, first_node * STEPS : (first_node + nodes) * STEPS],
            )

        for b in range(BLOCKS):
            for a in range(ADJ):
                load_a(b, a)

        for g in range(PASSES):
            flip_x(0, g)
            flip_x(1, g)
            sort_x(0, g, False)
            sort_x(1, g, True)
        flip_a(0, 0)
        sort_a(0, 0)
        negate_x(0)
        flip_x(2, 0)
        flip_a(0, 1)
        sort_a(0, 1)
        quantise_x(0)
        quantise_a(0, 0)
        flip_x(2, 1)
        flip_a(0, 2)
        sort_a(0, 2)
        permute_x(0)
        quantise_a(0, 1)
        flip_x(3, 0)
        flip_a(0, 3)
        sort_a(0, 3)
        flip_x(3, 1)
        quantise_a(0, 2)
        quantise_a(0, 3)
        negate_x(1)

        units = [("a", 1, a) for a in range(ADJ)] + [("a", 2, a) for a in range(ADJ)]
        units.extend(("a", 3, a) for a in range(ADJ))
        steps = []
        for i in range(PAIRS):
            steps.extend((i, b) for b in range(i))
            steps.extend((w, i) for w in range(i + 1))

        def flip(unit):
            kind, i, a = unit
            if kind == "x":
                for g in range(PASSES):
                    flip_x(i, g)
            else:
                flip_a(i, a)

        def sort(unit):
            kind, i, a = unit
            if kind == "x":
                for g in range(PASSES):
                    sort_x(i, g, False)
            else:
                sort_a(i, a)

        def finish(unit):
            kind, i, a = unit
            if kind == "x":
                negate_x(i)
                quantise_x(i)
                permute_x(i)
            else:
                quantise_a(i, a)

        last = len(steps) - 1
        for i, step in enumerate(steps):
            run = units[RUN * i : RUN * (i + 1)]
            for unit in run:
                flip(unit)
            for unit in run:
                sort(unit)
            if i == 0:
                quantise_x(1)
                permute_x(1)
                sort(("x", 2, 0))
            if i < last:
                multiply(*step)
            else:
                multiply(*step, first_node=0, nodes=BLOCK // 2)
            if i > 0:
                empty(*steps[i - 1], on_vector=(i % 2 == 0 or RUN * i < len(units)))
            for unit in run:
                finish(unit)
            if i == 1:
                finish(("x", 2, 0))
                sort(("x", 3, 0))
            if i == 3:
                finish(("x", 3, 0))
        multiply(*steps[last], first_node=BLOCK // 2, nodes=BLOCK // 2)
        empty(*steps[last], on_vector=True, first_node=0, nodes=BLOCK // 2)
        empty(*steps[last], on_vector=False, first_node=BLOCK // 2, nodes=BLOCK // 2, pieces=2)
